import numpy as np
import ml_dtypes


def mxq(x, axis, fmt="e4m3"):
    dtype, down = {"e4m3": (ml_dtypes.float8_e4m3fn, 7), "e5m2": (ml_dtypes.float8_e5m2, 14)}[fmt]
    v = np.moveaxis(np.asarray(x, np.float32).astype(ml_dtypes.bfloat16).astype(np.float64), axis, -1)
    blocks = v.reshape(v.shape[:-1] + (-1, 32))
    amax = np.abs(blocks).max(-1, keepdims=True)
    byte = np.maximum(np.where(amax > 0, np.frexp(amax)[1] - 1 + 127, 0) - down, 1)
    scale = np.exp2(byte - 127.0)
    codes = (blocks / scale).astype(np.float32).astype(dtype).astype(np.float64)
    return np.moveaxis((codes * scale).reshape(v.shape), -1, axis)


WIDE = False


def mx_kscale(k):
    if not WIDE:
        return np.ones(k)
    levels = np.array([10, -10, 5, -5, 0])
    a = np.random.permutation(np.resize(levels, k // 512 * 4)).reshape(k // 512, 4)
    idx = np.arange(k)
    return np.exp2(a[idx // 512, idx % 128 // 32])


BF16 = ml_dtypes.bfloat16


def bf(x):
    return np.asarray(x, np.float32).astype(BF16)


def f64(x):
    return np.asarray(x).astype(np.float64)


B, S, E, H, D, F = 2, 256, 1024, 8, 128, 4096
EPS = 1e-6
QUIET = 1e-3


def rmsnorm(x, scale):
    ms = np.mean(np.square(x), axis=-1, keepdims=True)
    return x * (1.0 / np.sqrt(ms + EPS)) * scale


def setup_inputs():
    s = mx_kscale(E)
    amp = np.where(np.random.random((B, S, 1)) < 0.25, QUIET, 1.0)
    return {"x": bf(np.random.standard_normal((B, S, E)) * amp),
            "scale1": bf(np.random.standard_normal(E) * s),
            "w_qkv": bf(np.random.standard_normal((E, H, 3 * D)) / np.sqrt(E) / s[:, None, None])}


def reference(x, scale1, w_qkv):
    xn = rmsnorm(f64(x), f64(scale1)).reshape(B * S, E)
    qkv = (mxq(xn, 1, "e4m3") @ mxq(f64(w_qkv).reshape(E, H * 3 * D), 0, "e4m3")).reshape(B, S, H, 3 * D)
    q, k, v = np.split(qkv, 3, axis=-1)
    return q, k, v

@@ -1,0 +1,201 @@
+from contextlib import ExitStack
+
+import concourse.mybir as mybir
+from concourse.masks import make_identity
+
+F32 = mybir.dt.float32
+BF16 = mybir.dt.bfloat16
+U32 = mybir.dt.uint32
+U8 = mybir.dt.uint8
+FP8X4 = mybir.dt.float8_e4m3fn_x4
+ACT = mybir.ActivationFunctionType
+ALU = mybir.AluOpType
+
+P = 128
+PACK = 4
+K_PASS = P * PACK
+
+ROWS = 512
+E = 1024
+HEADS = 8
+D = 128
+PARTS = 3
+EPS = 1e-6
+
+ROW_TILES = ROWS // P
+PASSES = E // K_PASS
+N_BLOCK = 512
+HEADS_PER_BLOCK = N_BLOCK // D
+HALVES = HEADS // HEADS_PER_BLOCK
+HALF_COLS = HEADS_PER_BLOCK * PARTS * D
+RUN = 4
+
+FLOPS = 2 * ROWS * E * HEADS * PARTS * D
+
+
+def tile_block_pa_kernel(tc, x, scale1, w_qkv, out_0, out_1, out_2):
+    nc = tc.nc
+    x_rows = x.rearrange("b s e -> (b s) e")
+    w_rows = w_qkv.rearrange("e h c -> e (h c)")
+    out_rows = [o.rearrange("b s h d -> (b s) (h d)") for o in (out_0, out_1, out_2)]
+
+    with ExitStack() as ctx:
+        consts = ctx.enter_context(tc.tile_pool(name="consts", bufs=1))
+        x_pool = ctx.enter_context(tc.tile_pool(name="x_pool", bufs=ROW_TILES))
+        w_pool = ctx.enter_context(tc.tile_pool(name="w_pool", bufs=PASSES * HALVES))
+        mx_pool = ctx.enter_context(tc.tile_pool(name="mx_pool", bufs=1))
+        stage = ctx.enter_context(tc.tile_pool(name="stage", bufs=3))
+        res_pool = ctx.enter_context(tc.tile_pool(name="res_pool", bufs=8))
+        psum = ctx.enter_context(tc.psum_pool(name="psum", bufs=8))
+
+        gain_row = consts.tile([P, E], BF16)
+        nc.vector.memset(gain_row[:], 0.0)
+        nc.sync.dma_start(out=gain_row[0:1, :], in_=scale1.unsqueeze(0))
+        eps = consts.tile([P, 1], F32)
+        nc.vector.memset(eps[:], EPS)
+        table_warm = consts.tile([P, 1], F32)
+        nc.scalar.activation(out=table_warm[:], in_=eps[:], func=ACT.Sqrt)
+
+        ident = consts.tile([P, P], BF16)
+        make_identity(nc, ident[:])
+        ones = consts.tile([P, P], BF16)
+        nc.vector.memset(ones[:], 1.0)
+
+        x_tiles = []
+        for m in range(ROW_TILES):
+            x_sb = x_pool.tile([P, E], BF16)
+            nc.sync.dma_start(out=x_sb[:], in_=x_rows[m * P : (m + 1) * P, :])
+            x_tiles.append(x_sb)
+        w_raw = {}
+        for half in range(HALVES):
+            for g in range(PASSES):
+                w_sb = w_pool.tile([P, PACK, HALF_COLS], BF16)
+                nc.sync.dma_start(
+                    out=w_sb[:],
+                    in_=w_rows[
+                        g * K_PASS : (g + 1) * K_PASS, half * HALF_COLS : (half + 1) * HALF_COLS
+                    ].rearrange("(t p) n -> p t n", p=P),
+                )
+                w_raw[(half, g)] = w_sb
+
+        gain = consts.tile([P, E], BF16)
+        for j in range(E // N_BLOCK):
+            cols = slice(j * N_BLOCK, (j + 1) * N_BLOCK)
+            spread = psum.tile([P, N_BLOCK], F32, tag="bank")
+            nc.tensor.matmul(
+                out=spread[:], lhsT=ones[:], rhs=gain_row[:, cols], start=True, stop=True
+            )
+            nc.vector.tensor_copy(out=gain[:, cols], in_=spread[:])
+
+        x_codes = []
+        x_scales = []
+        for m in range(ROW_TILES):
+            x_sb = x_tiles[m]
+            squares = x_pool.tile([P, E], BF16)
+            sum_sq = x_pool.tile([P, 1], F32)
+            nc.scalar.activation(out=squares[:], in_=x_sb[:], func=ACT.Square, accum_out=sum_sq[:])
+            rms = x_pool.tile([P, 1], F32)
+            nc.scalar.activation(
+                out=rms[:], in_=sum_sq[:], func=ACT.Sqrt, scale=1.0 / E, bias=eps[:]
+            )
+            inv_rms = x_pool.tile([P, 1], F32)
+            nc.vector.reciprocal(out=inv_rms[:], in_=rms[:])
+            xn = x_pool.tile([P, E], BF16)
+            nc.vector.scalar_tensor_tensor(
+                out=xn[:], in0=x_sb[:], scalar=inv_rms[:], in1=gain[:], op0=ALU.mult, op1=ALU.mult
+            )
+            x_grouped = x_pool.tile([P, PASSES, P, PACK], BF16, align_bytes=64)
+            for g in range(PASSES):
+                xt = psum.tile([P, PACK, P], BF16, tag="bank")
+                for t in range(PACK):
+                    first = g * K_PASS + t * P
+                    nc.tensor.transpose(xt[:, t, :], xn[:, first : first + P], ident[:])
+                nc.scalar.copy(out=x_grouped[:, g, :, :], in_=xt[:].rearrange("p t r -> p r t"))
+            codes = mx_pool.tile([P, PASSES, P], U32, name="x_codes%d" % m, align_bytes=64)
+            scales = mx_pool.tile([P, PASSES, P], U8, name="x_scales%d" % m, align_bytes=64)
+            nc.vector.quantize_mx(
+                out=codes[:].rearrange("p g r -> p (g r)").bitcast(FP8X4),
+                scales=scales[:].rearrange("p g r -> p (g r)"),
+                in_=x_grouped[:].rearrange("p g r t -> p (g r t)"),
+            )
+            x_codes.append(codes)
+            x_scales.append(scales)
+
+        units = [
+            (half, part, g)
+            for half in range(HALVES)
+            for part in range(PARTS)
+            for g in range(PASSES)
+        ]
+        w_grouped = {}
+        w_codes = {}
+        w_scales = {}
+        acc = {}
+
+        def regroup(unit):
+            half, part, g = unit
+            if part == PARTS - 1 and g == PASSES - 1:
+                grouped = stage.tile([P, N_BLOCK, PACK], BF16, name="by_scalar", align_bytes=64)
+                nc.scalar.copy(
+                    out=grouped[:].rearrange("p (h d) t -> p h d t", h=HEADS_PER_BLOCK),
+                    in_=w_raw[(half, g)][:].rearrange(
+                        "p t (h c d) -> p c h d t", h=HEADS_PER_BLOCK, c=PARTS
+                    )[:, part],
+                )
+            else:
+                grouped = stage.tile([P, N_BLOCK, PACK], BF16, name="by_vector", align_bytes=64)
+                nc.vector.tensor_copy(
+                    out=grouped[:].rearrange("p (h e i) t -> p h e t i", h=HEADS_PER_BLOCK, i=RUN),
+                    in_=w_raw[(half, g)][:].rearrange(
+                        "p t (h c e i) -> p c h e t i", h=HEADS_PER_BLOCK, c=PARTS, i=RUN
+                    )[:, part],
+                )
+            w_grouped[unit] = grouped
+
+        def quantise(unit):
+            codes = mx_pool.tile([P, N_BLOCK], U32, name="w_codes%d%d%d" % unit, align_bytes=64)
+            scales = mx_pool.tile([P, N_BLOCK], U8, name="w_scales%d%d%d" % unit, align_bytes=64)
+            nc.vector.quantize_mx(
+                out=codes[:].bitcast(FP8X4),
+                scales=scales[:],
+                in_=w_grouped[unit][:].rearrange("p n t -> p (n t)"),
+            )
+            w_codes[unit] = codes
+            w_scales[unit] = scales
+
+        def multiply(unit):
+            g = unit[2]
+            for m in range(ROW_TILES):
+                if g == 0:
+                    acc[m] = psum.tile([P, N_BLOCK], F32, name="acc", tag="bank")
+                nc.tensor.matmul_mx(
+                    out=acc[m][:],
+                    lhsT=x_codes[m][:, g, :].bitcast(FP8X4),
+                    lhsT_scale=x_scales[m][:, g, :],
+                    rhs=w_codes[unit][:].bitcast(FP8X4),
+                    rhs_scale=w_scales[unit][:],
+                    start=(g == 0),
+                    stop=(g == PASSES - 1),
+                )
+
+        def empty_and_store(unit):
+            half, part, g = unit
+            for m in range(ROW_TILES):
+                res = res_pool.tile([P, N_BLOCK], F32)
+                if unit == units[-1] and m % 2 == 1:
+                    nc.vector.tensor_copy(out=res[:], in_=acc[m][:])
+                else:
+                    nc.scalar.copy(out=res[:], in_=acc[m][:])
+                nc.sync.dma_start(
+                    out=out_rows[part][m * P : (m + 1) * P, half * N_BLOCK : (half + 1) * N_BLOCK],
+                    in_=res[:],
+                )
+
+        regroup(units[0])
+        for i, unit in enumerate(units):
+            if i + 1 < len(units):
+                regroup(units[i + 1])
+            quantise(unit)
+            multiply(unit)
+            if unit[2] == PASSES - 1:
+                empty_and_store(unit)

@@ -29,6 +29,7 @@ HEADS_PER_BLOCK = N_BLOCK // D
 HALVES = HEADS // HEADS_PER_BLOCK
 HALF_COLS = HEADS_PER_BLOCK * PARTS * D
 RUN = 4
+AHEAD = 2
 
 FLOPS = 2 * ROWS * E * HEADS * PARTS * D
 
@@ -40,6 +41,7 @@ def tile_block_pa_kernel(tc, x, scale1, w_qkv, out_0, out_1, out_2):
     out_rows = [o.rearrange("b s h d -> (b s) (h d)") for o in (out_0, out_1, out_2)]
 
     with ExitStack() as ctx:
+        ctx.enter_context(tc.manual_schedule())
         consts = ctx.enter_context(tc.tile_pool(name="consts", bufs=1))
         x_pool = ctx.enter_context(tc.tile_pool(name="x_pool", bufs=ROW_TILES))
         w_pool = ctx.enter_context(tc.tile_pool(name="w_pool", bufs=PASSES * HALVES))
@@ -87,8 +89,7 @@ def tile_block_pa_kernel(tc, x, scale1, w_qkv, out_0, out_1, out_2):
             )
             nc.vector.tensor_copy(out=gain[:, cols], in_=spread[:])
 
-        x_codes = []
-        x_scales = []
+        xt = []
         for m in range(ROW_TILES):
             x_sb = x_tiles[m]
             squares = x_pool.tile([P, E], BF16)
@@ -104,22 +105,12 @@ def tile_block_pa_kernel(tc, x, scale1, w_qkv, out_0, out_1, out_2):
             nc.vector.scalar_tensor_tensor(
                 out=xn[:], in0=x_sb[:], scalar=inv_rms[:], in1=gain[:], op0=ALU.mult, op1=ALU.mult
             )
-            x_grouped = x_pool.tile([P, PASSES, P, PACK], BF16, align_bytes=64)
+            xt_m = psum.tile([P, PASSES, PACK, P], BF16, tag="bank")
             for g in range(PASSES):
-                xt = psum.tile([P, PACK, P], BF16, tag="bank")
                 for t in range(PACK):
                     first = g * K_PASS + t * P
-                    nc.tensor.transpose(xt[:, t, :], xn[:, first : first + P], ident[:])
-                nc.scalar.copy(out=x_grouped[:, g, :, :], in_=xt[:].rearrange("p t r -> p r t"))
-            codes = mx_pool.tile([P, PASSES, P], U32, name="x_codes%d" % m, align_bytes=64)
-            scales = mx_pool.tile([P, PASSES, P], U8, name="x_scales%d" % m, align_bytes=64)
-            nc.vector.quantize_mx(
-                out=codes[:].rearrange("p g r -> p (g r)").bitcast(FP8X4),
-                scales=scales[:].rearrange("p g r -> p (g r)"),
-                in_=x_grouped[:].rearrange("p g r t -> p (g r t)"),
-            )
-            x_codes.append(codes)
-            x_scales.append(scales)
+                    nc.tensor.transpose(xt_m[:, g, t, :], xn[:, first : first + P], ident[:])
+            xt.append(xt_m)
 
         units = [
             (half, part, g)
@@ -127,6 +118,9 @@ def tile_block_pa_kernel(tc, x, scale1, w_qkv, out_0, out_1, out_2):
             for part in range(PARTS)
             for g in range(PASSES)
         ]
+        scalar_unit = (0, PARTS - 1, PASSES - 1)
+        x_codes = []
+        x_scales = []
         w_grouped = {}
         w_codes = {}
         w_scales = {}
@@ -134,8 +128,8 @@ def tile_block_pa_kernel(tc, x, scale1, w_qkv, out_0, out_1, out_2):
 
         def regroup(unit):
             half, part, g = unit
-            if part == PARTS - 1 and g == PASSES - 1:
-                grouped = stage.tile([P, N_BLOCK, PACK], BF16, name="by_scalar", align_bytes=64)
+            if unit == scalar_unit:
+                grouped = consts.tile([P, N_BLOCK, PACK], BF16, name="by_scalar", align_bytes=64)
                 nc.scalar.copy(
                     out=grouped[:].rearrange("p (h d) t -> p h d t", h=HEADS_PER_BLOCK),
                     in_=w_raw[(half, g)][:].rearrange(
@@ -179,7 +173,7 @@ def tile_block_pa_kernel(tc, x, scale1, w_qkv, out_0, out_1, out_2):
                 )
 
         def empty_and_store(unit):
-            half, part, g = unit
+            half, part = unit[0], unit[1]
             for m in range(ROW_TILES):
                 res = res_pool.tile([P, N_BLOCK], F32)
                 if unit == units[-1] and m % 2 == 1:
@@ -191,10 +185,27 @@ def tile_block_pa_kernel(tc, x, scale1, w_qkv, out_0, out_1, out_2):
                     in_=res[:],
                 )
 
-        regroup(units[0])
+        def quantise_x(m):
+            x_grouped = x_pool.tile([P, PASSES, P, PACK], BF16, align_bytes=64)
+            nc.scalar.copy(out=x_grouped[:], in_=xt[m][:].rearrange("p g t r -> p g r t"))
+            codes = mx_pool.tile([P, PASSES, P], U32, name="x_codes%d" % m, align_bytes=64)
+            scales = mx_pool.tile([P, PASSES, P], U8, name="x_scales%d" % m, align_bytes=64)
+            nc.vector.quantize_mx(
+                out=codes[:].rearrange("p g r -> p (g r)").bitcast(FP8X4),
+                scales=scales[:].rearrange("p g r -> p (g r)"),
+                in_=x_grouped[:].rearrange("p g r t -> p (g r t)"),
+            )
+            x_codes.append(codes)
+            x_scales.append(scales)
+
+        for unit in units[:AHEAD]:
+            regroup(unit)
+        for m in range(ROW_TILES):
+            quantise_x(m)
+        regroup(scalar_unit)
         for i, unit in enumerate(units):
-            if i + 1 < len(units):
-                regroup(units[i + 1])
+            if i + AHEAD < len(units) and units[i + AHEAD] != scalar_unit:
+                regroup(units[i + AHEAD])
             quantise(unit)
             multiply(unit)
             if unit[2] == PASSES - 1:

@@ -5,6 +5,7 @@ from concourse.masks import make_identity
 
 F32 = mybir.dt.float32
 BF16 = mybir.dt.bfloat16
+I32 = mybir.dt.int32
 U32 = mybir.dt.uint32
 U8 = mybir.dt.uint8
 FP8X4 = mybir.dt.float8_e4m3fn_x4
@@ -51,8 +52,7 @@ def tile_block_pa_kernel(tc, x, scale1, w_qkv, out_0, out_1, out_2):
         psum = ctx.enter_context(tc.psum_pool(name="psum", bufs=8))
 
         gain_row = consts.tile([P, E], BF16)
-        nc.vector.memset(gain_row[:], 0.0)
-        nc.sync.dma_start(out=gain_row[0:1, :], in_=scale1.unsqueeze(0))
+        nc.vector.memset(gain_row[:].bitcast(I32), 0)
         eps = consts.tile([P, 1], F32)
         nc.vector.memset(eps[:], EPS)
         table_warm = consts.tile([P, 1], F32)
@@ -68,6 +68,8 @@ def tile_block_pa_kernel(tc, x, scale1, w_qkv, out_0, out_1, out_2):
             x_sb = x_pool.tile([P, E], BF16)
             nc.sync.dma_start(out=x_sb[:], in_=x_rows[m * P : (m + 1) * P, :])
             x_tiles.append(x_sb)
+            if m == 0:
+                nc.sync.dma_start(out=gain_row[0:1, :], in_=scale1.unsqueeze(0))
         w_raw = {}
         for half in range(HALVES):
             for g in range(PASSES):
@@ -80,14 +82,17 @@ def tile_block_pa_kernel(tc, x, scale1, w_qkv, out_0, out_1, out_2):
                 )
                 w_raw[(half, g)] = w_sb
 
-        gain = consts.tile([P, E], BF16)
-        for j in range(E // N_BLOCK):
-            cols = slice(j * N_BLOCK, (j + 1) * N_BLOCK)
-            spread = psum.tile([P, N_BLOCK], F32, tag="bank")
+        gain = []
+        for g in range(PASSES):
+            spread = psum.tile([P, K_PASS], F32, tag="bank")
             nc.tensor.matmul(
-                out=spread[:], lhsT=ones[:], rhs=gain_row[:, cols], start=True, stop=True
+                out=spread[:],
+                lhsT=ones[:],
+                rhs=gain_row[:, g * K_PASS : (g + 1) * K_PASS],
+                start=True,
+                stop=True,
             )
-            nc.vector.tensor_copy(out=gain[:, cols], in_=spread[:])
+            gain.append(spread)
 
         xt = []
         for m in range(ROW_TILES):
@@ -102,9 +107,16 @@ def tile_block_pa_kernel(tc, x, scale1, w_qkv, out_0, out_1, out_2):
             inv_rms = x_pool.tile([P, 1], F32)
             nc.vector.reciprocal(out=inv_rms[:], in_=rms[:])
             xn = x_pool.tile([P, E], BF16)
-            nc.vector.scalar_tensor_tensor(
-                out=xn[:], in0=x_sb[:], scalar=inv_rms[:], in1=gain[:], op0=ALU.mult, op1=ALU.mult
-            )
+            for g in range(PASSES):
+                cols = slice(g * K_PASS, (g + 1) * K_PASS)
+                nc.vector.scalar_tensor_tensor(
+                    out=xn[:, cols],
+                    in0=x_sb[:, cols],
+                    scalar=inv_rms[:],
+                    in1=gain[g][:],
+                    op0=ALU.mult,
+                    op1=ALU.mult,
+                )
             xt_m = psum.tile([P, PASSES, PACK, P], BF16, tag="bank")
             for g in range(PASSES):
                 for t in range(PACK):
@@ -118,7 +130,7 @@ def tile_block_pa_kernel(tc, x, scale1, w_qkv, out_0, out_1, out_2):
             for part in range(PARTS)
             for g in range(PASSES)
         ]
-        scalar_unit = (0, PARTS - 1, PASSES - 1)
+        scalar_units = [(half, PARTS - 1, PASSES - 1) for half in range(HALVES)]
         x_codes = []
         x_scales = []
         w_grouped = {}
@@ -128,8 +140,8 @@ def tile_block_pa_kernel(tc, x, scale1, w_qkv, out_0, out_1, out_2):
 
         def regroup(unit):
             half, part, g = unit
-            if unit == scalar_unit:
-                grouped = consts.tile([P, N_BLOCK, PACK], BF16, name="by_scalar", align_bytes=64)
+            if unit in scalar_units:
+                grouped = stage.tile([P, N_BLOCK, PACK], BF16, name="by_scalar", align_bytes=64)
                 nc.scalar.copy(
                     out=grouped[:].rearrange("p (h d) t -> p h d t", h=HEADS_PER_BLOCK),
                     in_=w_raw[(half, g)][:].rearrange(
@@ -202,9 +214,10 @@ def tile_block_pa_kernel(tc, x, scale1, w_qkv, out_0, out_1, out_2):
             regroup(unit)
         for m in range(ROW_TILES):
             quantise_x(m)
-        regroup(scalar_unit)
         for i, unit in enumerate(units):
-            if i + AHEAD < len(units) and units[i + AHEAD] != scalar_unit:
+            if unit[1] == 0 and unit[2] == 0:
+                regroup(scalar_units[unit[0]])
+            if i + AHEAD < len(units) and units[i + AHEAD] not in scalar_units:
                 regroup(units[i + AHEAD])
             quantise(unit)
             multiply(unit)

from contextlib import ExitStack

import concourse.mybir as mybir
from concourse.masks import make_identity

F32 = mybir.dt.float32
BF16 = mybir.dt.bfloat16
I32 = mybir.dt.int32
U32 = mybir.dt.uint32
U8 = mybir.dt.uint8
FP8X4 = mybir.dt.float8_e4m3fn_x4
ACT = mybir.ActivationFunctionType
ALU = mybir.AluOpType

P = 128
PACK = 4
K_PASS = P * PACK

ROWS = 512
E = 1024
HEADS = 8
D = 128
PARTS = 3
EPS = 1e-6

ROW_TILES = ROWS // P
PASSES = E // K_PASS
N_BLOCK = 512
HEADS_PER_BLOCK = N_BLOCK // D
HALVES = HEADS // HEADS_PER_BLOCK
HALF_COLS = HEADS_PER_BLOCK * PARTS * D
RUN = 4
AHEAD = 2

FLOPS = 2 * ROWS * E * HEADS * PARTS * D


def tile_block_pa_kernel(tc, x, scale1, w_qkv, out_0, out_1, out_2):
    nc = tc.nc
    x_rows = x.rearrange("b s e -> (b s) e")
    w_rows = w_qkv.rearrange("e h c -> e (h c)")
    out_rows = [o.rearrange("b s h d -> (b s) (h d)") for o in (out_0, out_1, out_2)]

    with ExitStack() as ctx:
        ctx.enter_context(tc.manual_schedule())
        consts = ctx.enter_context(tc.tile_pool(name="consts", bufs=1))
        x_pool = ctx.enter_context(tc.tile_pool(name="x_pool", bufs=ROW_TILES))
        w_pool = ctx.enter_context(tc.tile_pool(name="w_pool", bufs=PASSES * HALVES))
        mx_pool = ctx.enter_context(tc.tile_pool(name="mx_pool", bufs=1))
        stage = ctx.enter_context(tc.tile_pool(name="stage", bufs=3))
        res_pool = ctx.enter_context(tc.tile_pool(name="res_pool", bufs=8))
        psum = ctx.enter_context(tc.psum_pool(name="psum", bufs=8))

        gain_row = consts.tile([P, E], BF16)
        nc.vector.memset(gain_row[:].bitcast(I32), 0)
        eps = consts.tile([P, 1], F32)
        nc.vector.memset(eps[:], EPS)
        table_warm = consts.tile([P, 1], F32)
        nc.scalar.activation(out=table_warm[:], in_=eps[:], func=ACT.Sqrt)

        ident = consts.tile([P, P], BF16)
        make_identity(nc, ident[:])
        ones = consts.tile([P, P], BF16)
        nc.vector.memset(ones[:], 1.0)

        x_tiles = []
        for m in range(ROW_TILES):
            x_sb = x_pool.tile([P, E], BF16)
            nc.sync.dma_start(out=x_sb[:], in_=x_rows[m * P : (m + 1) * P, :])
            x_tiles.append(x_sb)
            if m == 0:
                nc.sync.dma_start(out=gain_row[0:1, :], in_=scale1.unsqueeze(0))
        w_raw = {}
        for half in range(HALVES):
            for g in range(PASSES):
                w_sb = w_pool.tile([P, PACK, HALF_COLS], BF16)
                nc.sync.dma_start(
                    out=w_sb[:],
                    in_=w_rows[
                        g * K_PASS : (g + 1) * K_PASS, half * HALF_COLS : (half + 1) * HALF_COLS
                    ].rearrange("(t p) n -> p t n", p=P),
                )
                w_raw[(half, g)] = w_sb

        gain = []
        for g in range(PASSES):
            spread = psum.tile([P, K_PASS], F32, tag="bank")
            nc.tensor.matmul(
                out=spread[:],
                lhsT=ones[:],
                rhs=gain_row[:, g * K_PASS : (g + 1) * K_PASS],
                start=True,
                stop=True,
            )
            gain.append(spread)

        xt = []
        for m in range(ROW_TILES):
            x_sb = x_tiles[m]
            squares = x_pool.tile([P, E], BF16)
            sum_sq = x_pool.tile([P, 1], F32)
            nc.scalar.activation(out=squares[:], in_=x_sb[:], func=ACT.Square, accum_out=sum_sq[:])
            rms = x_pool.tile([P, 1], F32)
            nc.scalar.activation(
                out=rms[:], in_=sum_sq[:], func=ACT.Sqrt, scale=1.0 / E, bias=eps[:]
            )
            inv_rms = x_pool.tile([P, 1], F32)
            nc.vector.reciprocal(out=inv_rms[:], in_=rms[:])
            xn = x_pool.tile([P, E], BF16)
            for g in range(PASSES):
                cols = slice(g * K_PASS, (g + 1) * K_PASS)
                nc.vector.scalar_tensor_tensor(
                    out=xn[:, cols],
                    in0=x_sb[:, cols],
                    scalar=inv_rms[:],
                    in1=gain[g][:],
                    op0=ALU.mult,
                    op1=ALU.mult,
                )
            xt_m = psum.tile([P, PASSES, PACK, P], BF16, tag="bank")
            for g in range(PASSES):
                for t in range(PACK):
                    first = g * K_PASS + t * P
                    nc.tensor.transpose(xt_m[:, g, t, :], xn[:, first : first + P], ident[:])
            xt.append(xt_m)

        units = [
            (half, part, g)
            for half in range(HALVES)
            for part in range(PARTS)
            for g in range(PASSES)
        ]
        scalar_units = [(half, PARTS - 1, PASSES - 1) for half in range(HALVES)]
        x_codes = []
        x_scales = []
        w_grouped = {}
        w_codes = {}
        w_scales = {}
        acc = {}

        def regroup(unit):
            half, part, g = unit
            if unit in scalar_units:
                grouped = stage.tile([P, N_BLOCK, PACK], BF16, name="by_scalar", align_bytes=64)
                nc.scalar.copy(
                    out=grouped[:].rearrange("p (h d) t -> p h d t", h=HEADS_PER_BLOCK),
                    in_=w_raw[(half, g)][:].rearrange(
                        "p t (h c d) -> p c h d t", h=HEADS_PER_BLOCK, c=PARTS
                    )[:, part],
                )
            else:
                grouped = stage.tile([P, N_BLOCK, PACK], BF16, name="by_vector", align_bytes=64)
                nc.vector.tensor_copy(
                    out=grouped[:].rearrange("p (h e i) t -> p h e t i", h=HEADS_PER_BLOCK, i=RUN),
                    in_=w_raw[(half, g)][:].rearrange(
                        "p t (h c e i) -> p c h e t i", h=HEADS_PER_BLOCK, c=PARTS, i=RUN
                    )[:, part],
                )
            w_grouped[unit] = grouped

        def quantise(unit):
            codes = mx_pool.tile([P, N_BLOCK], U32, name="w_codes%d%d%d" % unit, align_bytes=64)
            scales = mx_pool.tile([P, N_BLOCK], U8, name="w_scales%d%d%d" % unit, align_bytes=64)
            nc.vector.quantize_mx(
                out=codes[:].bitcast(FP8X4),
                scales=scales[:],
                in_=w_grouped[unit][:].rearrange("p n t -> p (n t)"),
            )
            w_codes[unit] = codes
            w_scales[unit] = scales

        def multiply(unit):
            g = unit[2]
            for m in range(ROW_TILES):
                if g == 0:
                    acc[m] = psum.tile([P, N_BLOCK], F32, name="acc", tag="bank")
                nc.tensor.matmul_mx(
                    out=acc[m][:],
                    lhsT=x_codes[m][:, g, :].bitcast(FP8X4),
                    lhsT_scale=x_scales[m][:, g, :],
                    rhs=w_codes[unit][:].bitcast(FP8X4),
                    rhs_scale=w_scales[unit][:],
                    start=(g == 0),
                    stop=(g == PASSES - 1),
                )

        def empty_and_store(unit):
            half, part = unit[0], unit[1]
            for m in range(ROW_TILES):
                res = res_pool.tile([P, N_BLOCK], F32)
                if unit == units[-1] and m % 2 == 1:
                    nc.vector.tensor_copy(out=res[:], in_=acc[m][:])
                else:
                    nc.scalar.copy(out=res[:], in_=acc[m][:])
                nc.sync.dma_start(
                    out=out_rows[part][m * P : (m + 1) * P, half * N_BLOCK : (half + 1) * N_BLOCK],
                    in_=res[:],
                )

        def quantise_x(m):
            x_grouped = x_pool.tile([P, PASSES, P, PACK], BF16, align_bytes=64)
            nc.scalar.copy(out=x_grouped[:], in_=xt[m][:].rearrange("p g t r -> p g r t"))
            codes = mx_pool.tile([P, PASSES, P], U32, name="x_codes%d" % m, align_bytes=64)
            scales = mx_pool.tile([P, PASSES, P], U8, name="x_scales%d" % m, align_bytes=64)
            nc.vector.quantize_mx(
                out=codes[:].rearrange("p g r -> p (g r)").bitcast(FP8X4),
                scales=scales[:].rearrange("p g r -> p (g r)"),
                in_=x_grouped[:].rearrange("p g r t -> p (g r t)"),
            )
            x_codes.append(codes)
            x_scales.append(scales)

        for unit in units[:AHEAD]:
            regroup(unit)
        for m in range(ROW_TILES):
            quantise_x(m)
        for i, unit in enumerate(units):
            if unit[1] == 0 and unit[2] == 0:
                regroup(scalar_units[unit[0]])
            if i + AHEAD < len(units) and units[i + AHEAD] not in scalar_units:
                regroup(units[i + AHEAD])
            quantise(unit)
            multiply(unit)
            if unit[2] == PASSES - 1:
                empty_and_store(unit)
